import numpy as np
import ml_dtypes


def mxq(x, axis, fmt="e4m3"):
    dtype, down = {"e4m3": (ml_dtypes.float8_e4m3fn, 7), "e5m2": (ml_dtypes.float8_e5m2, 14)}[fmt]
    v = np.moveaxis(np.asarray(x, np.float32).astype(ml_dtypes.bfloat16).astype(np.float64), axis, -1)
    blocks = v.reshape(v.shape[:-1] + (-1, 32))
    amax = np.abs(blocks).max(-1, keepdims=True)
    byte = np.maximum(np.where(amax > 0, np.frexp(amax)[1] - 1 + 127, 0) - down, 1)
    scale = np.exp2(byte - 127.0)
    codes = (blocks / scale).astype(np.float32).astype(dtype).astype(np.float64)
    return np.moveaxis((codes * scale).reshape(v.shape), -1, axis)


WIDE = False


def mx_kscale(k):
    if not WIDE:
        return np.ones(k)
    levels = np.array([10, -10, 5, -5, 0])
    a = np.random.permutation(np.resize(levels, k // 512 * 4)).reshape(k // 512, 4)
    idx = np.arange(k)
    return np.exp2(a[idx // 512, idx % 128 // 32])


BF16 = ml_dtypes.bfloat16


def bf(x):
    return np.asarray(x, np.float32).astype(BF16)


def f64(x):
    return np.asarray(x).astype(np.float64)


B, D, H = 1024, 512, 1024


def sigmoid(v):
    return 1.0 / (1.0 + np.exp(-v))


def setup_inputs():
    s = mx_kscale(H)
    return {"h0": bf(np.random.standard_normal((B, H)) * 0.2 * s),
            "W_ih1": bf(np.random.standard_normal((4 * H, H)) * 6.0 / np.sqrt(H) / s[None, :]),
            "b_ih1": bf(np.random.standard_normal(4 * H) * 0.3),
            "b_hh1": bf(np.random.standard_normal(4 * H) * 0.3),
            "W_dec": bf(np.random.standard_normal((D, H)) * 5.0 / np.sqrt(H)),
            "b_dec": bf(np.random.standard_normal(D) * 0.3)}


def reference(h0, W_ih1, b_ih1, b_hh1, W_dec, b_dec):
    w = f64(W_ih1)
    b = f64(b_ih1) + f64(b_hh1)
    hq = mxq(f64(h0), 1, "e4m3")
    a_i = (hq @ mxq(w[:H].T, 0, "e4m3")) + b[:H]
    a_g = (hq @ mxq(w[2 * H:3 * H].T, 0, "e4m3")) + b[2 * H:3 * H]
    a_o = (hq @ mxq(w[3 * H:].T, 0, "e4m3")) + b[3 * H:]
    c = sigmoid(a_i) * np.tanh(a_g)
    h1 = sigmoid(a_o) * np.tanh(c)
    return (mxq(h1, 1, "e4m3") @ mxq(f64(W_dec).T, 0, "e4m3")) + f64(b_dec)

@@ -1,0 +1,216 @@
+from contextlib import ExitStack
+
+import concourse.mybir as mybir
+from concourse.masks import make_identity
+
+B, H, D = 1024, 1024, 512
+FLOPS = 2 * B * H * (3 * H + D)
+BYTES = 2 * (B * H + 3 * H * H + 6 * H + D * H + D) + 4 * B * D
+
+F32 = mybir.dt.float32
+BF16 = mybir.dt.bfloat16
+U32 = mybir.dt.uint32
+U8 = mybir.dt.uint8
+FP8X4 = mybir.dt.float8_e4m3fn_x4
+ACT = mybir.ActivationFunctionType
+ALU = mybir.AluOpType
+
+P = 128
+NB = 512
+GATES = (0, 2, 3)
+
+
+def tile_lstmbaseline_pb_kernel(tc, h0, W_ih1, b_ih1, b_hh1, W_dec, b_dec, out):
+    nc = tc.nc
+    with ExitStack() as ctx:
+        consts = ctx.enter_context(tc.tile_pool(name="consts", bufs=1))
+        raw = ctx.enter_context(tc.tile_pool(name="raw", bufs=1))
+        stage = ctx.enter_context(tc.tile_pool(name="stage", bufs=3))
+        codes = ctx.enter_context(tc.tile_pool(name="codes", bufs=1))
+        act = ctx.enter_context(tc.tile_pool(name="act", bufs=3))
+        psum = ctx.enter_context(tc.psum_pool(name="psum", bufs=8))
+
+        ident = consts.tile([P, P], F32, name="ident")
+        make_identity(nc, ident[:])
+        warm = consts.tile([P, 2], F32, name="warm")
+        nc.vector.memset(warm[:], 0.0)
+        nc.scalar.activation(out=warm[:, 1:2], in_=warm[:, 0:1], func=ACT.Sigmoid)
+        brows = consts.tile([P, 256], BF16, name="brows")
+        nc.vector.memset(brows[:], 0.0)
+        nc.scalar.dma_start(out=brows[0:16, :], in_=b_ih1.rearrange("(r q) -> r q", q=256))
+        nc.scalar.dma_start(out=brows[16:32, :], in_=b_hh1.rearrange("(r q) -> r q", q=256))
+
+        h0raw = [raw.tile([P, 4, H], BF16, name="h0raw%d" % n) for n in range(2)]
+        wraw = {}
+        for g in range(2):
+            for u in range(2):
+                for gi in range(3):
+                    wraw[(gi, g, u)] = raw.tile([P, 2, H], BF16, name="wraw%d%d%d" % (gi, g, u))
+        wdraw = raw.tile([P, 4, H], BF16, name="wdraw")
+        bdec = consts.tile([P, D], BF16, name="bdec")
+
+        def load_h0(n):
+            view = h0[NB * n : NB * (n + 1), :].rearrange("(r a) k -> r a k", a=4)
+            for b in range(2):
+                nc.sync.dma_start(out=h0raw[n][:, 2 * b : 2 * b + 2, :], in_=view[:, 2 * b : 2 * b + 2, :])
+
+        def w_view(gi, g, u):
+            base = GATES[gi] * H + 512 * g + 256 * u
+            return W_ih1[base : base + 256, :].rearrange("(p e) k -> p e k", e=2)
+
+        load_h0(0)
+        for gi in range(3):
+            nc.sync.dma_start(out=wraw[(gi, 0, 0)][:, 0, :], in_=w_view(gi, 0, 0)[:, 0, :])
+        load_h0(1)
+        for gi in range(3):
+            nc.sync.dma_start(out=wraw[(gi, 0, 0)][:, 1, :], in_=w_view(gi, 0, 0)[:, 1, :])
+        for g, u in ((0, 1), (1, 0), (1, 1)):
+            for gi in range(3):
+                nc.sync.dma_start(out=wraw[(gi, g, u)][:], in_=w_view(gi, g, u))
+        wd_view = W_dec.rearrange("(a r) k -> r a k", r=P)
+        for b in range(2):
+            nc.sync.dma_start(out=wdraw[:, 2 * b : 2 * b + 2, :], in_=wd_view[:, 2 * b : 2 * b + 2, :])
+        nc.sync.dma_start(out=bdec[:], in_=b_dec.partition_broadcast(P))
+
+        def code_tiles(shape, name):
+            return (
+                codes.tile(shape, U32, name=name + "c", align_bytes=64),
+                codes.tile(shape, U8, name=name + "s", align_bytes=64),
+            )
+
+        h0q = {(c, n): code_tiles([P, NB], "h0q%d%d" % (c, n)) for c in range(2) for n in range(2)}
+        wq = {(g, t): code_tiles([P, 3, 2, P], "wq%d%d" % (g, t)) for g in range(2) for t in range(4)}
+        wdq = {c: code_tiles([P, D], "wdq%d" % c) for c in range(2)}
+        h1q = {(g, n): code_tiles([P, NB], "h1q%d%d" % (g, n)) for g in range(2) for n in range(2)}
+
+        def leave_psum(eng, dst, src):
+            if eng == "s":
+                nc.scalar.copy(out=dst, in_=src)
+            else:
+                nc.vector.tensor_copy(out=dst, in_=src)
+
+        def convert_moving(src, c, dst, engines):
+            words = src[:].bitcast(F32)
+            grp = stage.tile([P, 2048], BF16, name="grp2", tag="grp2", align_bytes=64)
+            grp_w = grp[:].bitcast(F32).rearrange("p (b a r v) -> p b a r v", b=2, a=2, v=2)
+            banks = []
+            for b in range(2):
+                bank = psum.tile([P, 2, 2, P], F32, name="bank", tag="bank")
+                banks.append(bank)
+                for a in range(2):
+                    for v in range(2):
+                        lo = 256 * c + 128 * v
+                        nc.tensor.transpose(out=bank[:, a, v, :], in_=words[:, 2 * b + a, lo : lo + P], identity=ident[:])
+            for b in range(2):
+                leave_psum(engines[b], grp_w[:, b], banks[b][:].rearrange("p a v r -> p a r v"))
+            nc.vector.quantize_mx(out=dst[0][:].bitcast(FP8X4), scales=dst[1][:], in_=grp[:])
+
+        def convert_weights(g, t, engines):
+            u, e = divmod(t, 2)
+            banks = []
+            for gi in range(3):
+                words = wraw[(gi, g, u)][:].bitcast(F32)
+                bank = psum.tile([P, 2, 2, P], F32, name="bank", tag="bank")
+                banks.append(bank)
+                for c in range(2):
+                    for v in range(2):
+                        lo = 256 * c + 128 * v
+                        nc.tensor.transpose(out=bank[:, c, v, :], in_=words[:, e, lo : lo + P], identity=ident[:])
+            grps = []
+            for gi in range(3):
+                grp = stage.tile([P, 1024], BF16, name="grp1", tag="grp1", bufs=6, align_bytes=64)
+                grps.append(grp)
+                grp_w = grp[:].bitcast(F32).rearrange("p (c r v) -> p c r v", c=2, v=2)
+                leave_psum(engines[gi], grp_w, banks[gi][:].rearrange("p c v r -> p c r v"))
+            for gi in range(3):
+                nc.vector.quantize_mx(
+                    out=wq[(g, t)][0][:, gi].rearrange("p c r -> p (c r)").bitcast(FP8X4),
+                    scales=wq[(g, t)][1][:, gi].rearrange("p c r -> p (c r)"),
+                    in_=grps[gi][:],
+                )
+
+        bsum = consts.tile([P, 32], F32, name="bsum")
+
+        def prepare_bias():
+            bank = psum.tile([P, 4, P], F32, name="bank", tag="bank")
+            nc.tensor.transpose(out=bank[:, 0, :], in_=brows[:].bitcast(F32), identity=ident[:])
+            bw = consts.tile([P, 64], BF16, name="bw")
+            nc.vector.tensor_copy(out=bw[:].bitcast(F32), in_=bank[:, 0, 0:32])
+            nc.vector.tensor_tensor(out=bsum[:], in0=bw[:, 0:32], in1=bw[:, 32:64], op=ALU.add)
+
+        h1p = {}
+
+        def unit(g, t, n):
+            accs = []
+            for gi in range(3):
+                acc = psum.tile([P, NB], F32, name="acc", tag="bank")
+                accs.append(acc)
+                for c in range(2):
+                    nc.tensor.matmul_mx(
+                        out=acc[:],
+                        lhsT=wq[(g, t)][0][:, gi, c, :].bitcast(FP8X4),
+                        lhsT_scale=wq[(g, t)][1][:, gi, c, :],
+                        rhs=h0q[(c, n)][0][:].bitcast(FP8X4),
+                        rhs_scale=h0q[(c, n)][1][:],
+                        start=(c == 0),
+                        stop=(c == 1),
+                    )
+            outs = []
+            for gi, func in enumerate((ACT.Sigmoid, ACT.Tanh, ACT.Sigmoid)):
+                col = GATES[gi] * 8 + g * 4 + t
+                o = act.tile([P, NB], F32, name="gate%d" % gi, tag="gate%d" % gi)
+                outs.append(o)
+                nc.scalar.activation(out=o[:], in_=accs[gi][:], func=func, bias=bsum[:, col : col + 1])
+            cc = act.tile([P, NB], F32, name="cc", tag="cc")
+            nc.vector.tensor_tensor(out=cc[:], in0=outs[0][:], in1=outs[1][:], op=ALU.mult)
+            tcc = act.tile([P, NB], F32, name="tcc", tag="tcc")
+            nc.scalar.activation(out=tcc[:], in_=cc[:], func=ACT.Tanh)
+            if t == 0:
+                h1p[n] = stage.tile([P, 4, NB], BF16, name="h1p", tag="h1p", bufs=4)
+            nc.vector.tensor_tensor(out=h1p[n][:, t, :], in0=outs[2][:], in1=tcc[:], op=ALU.mult)
+            if t == 3:
+                h1g = stage.tile([P, NB, 4], BF16, name="h1g", tag="h1g", bufs=2, align_bytes=64)
+                nc.vector.tensor_copy(
+                    out=h1g[:].rearrange("p (c i) t -> p c t i", i=4),
+                    in_=h1p[n][:].rearrange("p t (c i) -> p c t i", i=4),
+                )
+                nc.vector.quantize_mx(
+                    out=h1q[(g, n)][0][:].bitcast(FP8X4),
+                    scales=h1q[(g, n)][1][:],
+                    in_=h1g[:].rearrange("p c t -> p (c t)"),
+                )
+
+        def decode(n):
+            view = out[NB * n : NB * (n + 1), :].rearrange("(r a) d -> r a d", a=4)
+            for a in range(4):
+                acc = psum.tile([P, D], F32, name="acc", tag="bank")
+                for g in range(2):
+                    nc.tensor.matmul_mx(
+                        out=acc[:],
+                        lhsT=h1q[(g, n)][0][:, P * a : P * (a + 1)].bitcast(FP8X4),
+                        lhsT_scale=h1q[(g, n)][1][:, P * a : P * (a + 1)],
+                        rhs=wdq[g][0][:].bitcast(FP8X4),
+                        rhs_scale=wdq[g][1][:],
+                        start=(g == 0),
+                        stop=(g == 1),
+                    )
+                res = act.tile([P, D], F32, name="res", tag="res", bufs=4)
+                nc.vector.tensor_tensor(out=res[:], in0=acc[:], in1=bdec[:], op=ALU.add)
+                nc.sync.dma_start(out=view[:, a, :], in_=res[:])
+
+        convert_moving(h0raw[0], 0, h0q[(0, 0)], "sv")
+        convert_moving(h0raw[0], 1, h0q[(1, 0)], "sv")
+        convert_weights(0, 0, "svs")
+        prepare_bias()
+        convert_moving(h0raw[1], 0, h0q[(0, 1)], "sv")
+        convert_moving(h0raw[1], 1, h0q[(1, 1)], "sv")
+        pairs = [(g, t) for g in range(2) for t in range(4)]
+        for i, (g, t) in enumerate(pairs):
+            if i + 1 < len(pairs):
+                convert_weights(pairs[i + 1][0], pairs[i + 1][1], "vsv")
+            if i in (5, 6):
+                convert_moving(wdraw, i - 5, wdq[i - 5], "sv")
+            for n in range(2):
+                unit(g, t, n)
+                if (g, t) == (1, 3):
+                    decode(n)

@@ -18,6 +18,13 @@ ALU = mybir.AluOpType
 P = 128
 NB = 512
 GATES = (0, 2, 3)
+W_FIRST = 4
+UNITS = [(0, t, n, 0, 512) for t in range(4) for n in range(2)] + [(1, t, 0, 0, 512) for t in range(4)] + [(1, t, 1, 0, 512) for t in range(3)] + [(1, 3, 1, 0, 256), (1, 3, 1, 256, 256)]
+PRE = 6
+PRE_ENG = "vsssss"
+COPY_ENG = "svsvsvsvsvsv"
+RG0 = {11: 0, 14: 1}
+DLAG = 2
 
 
 def tile_lstmbaseline_pb_kernel(tc, h0, W_ih1, b_ih1, b_hh1, W_dec, b_dec, out):
@@ -41,11 +48,7 @@ def tile_lstmbaseline_pb_kernel(tc, h0, W_ih1, b_ih1, b_hh1, W_dec, b_dec, out):
         nc.scalar.dma_start(out=brows[16:32, :], in_=b_hh1.rearrange("(r q) -> r q", q=256))
 
         h0raw = [raw.tile([P, 4, H], BF16, name="h0raw%d" % n) for n in range(2)]
-        wraw = {}
-        for g in range(2):
-            for u in range(2):
-                for gi in range(3):
-                    wraw[(gi, g, u)] = raw.tile([P, 2, H], BF16, name="wraw%d%d%d" % (gi, g, u))
+        wraw = [raw.tile([P, H], BF16, name="wraw%d" % w) for w in range(24)]
         wdraw = raw.tile([P, 4, H], BF16, name="wdraw")
         bdec = consts.tile([P, D], BF16, name="bdec")
 
@@ -54,163 +57,200 @@ def tile_lstmbaseline_pb_kernel(tc, h0, W_ih1, b_ih1, b_hh1, W_dec, b_dec, out):
             for b in range(2):
                 nc.sync.dma_start(out=h0raw[n][:, 2 * b : 2 * b + 2, :], in_=view[:, 2 * b : 2 * b + 2, :])
 
-        def w_view(gi, g, u):
+        def load_w(w):
+            q, gi = divmod(w, 3)
+            g, t = divmod(q, 4)
+            u, e = divmod(t, 2)
             base = GATES[gi] * H + 512 * g + 256 * u
-            return W_ih1[base : base + 256, :].rearrange("(p e) k -> p e k", e=2)
+            nc.sync.dma_start(out=wraw[w][:], in_=W_ih1[base : base + 256, :].rearrange("(p e) k -> p e k", e=2)[:, e, :])
 
         load_h0(0)
-        for gi in range(3):
-            nc.sync.dma_start(out=wraw[(gi, 0, 0)][:, 0, :], in_=w_view(gi, 0, 0)[:, 0, :])
+        for w in range(W_FIRST):
+            load_w(w)
         load_h0(1)
-        for gi in range(3):
-            nc.sync.dma_start(out=wraw[(gi, 0, 0)][:, 1, :], in_=w_view(gi, 0, 0)[:, 1, :])
-        for g, u in ((0, 1), (1, 0), (1, 1)):
-            for gi in range(3):
-                nc.sync.dma_start(out=wraw[(gi, g, u)][:], in_=w_view(gi, g, u))
+        for w in range(W_FIRST, 24):
+            load_w(w)
         wd_view = W_dec.rearrange("(a r) k -> r a k", r=P)
         for b in range(2):
             nc.sync.dma_start(out=wdraw[:, 2 * b : 2 * b + 2, :], in_=wd_view[:, 2 * b : 2 * b + 2, :])
         nc.sync.dma_start(out=bdec[:], in_=b_dec.partition_broadcast(P))
 
-        def code_tiles(shape, name):
+        def code_tiles(name):
             return (
-                codes.tile(shape, U32, name=name + "c", align_bytes=64),
-                codes.tile(shape, U8, name=name + "s", align_bytes=64),
+                codes.tile([P, NB], U32, name=name + "c", align_bytes=64),
+                codes.tile([P, NB], U8, name=name + "s", align_bytes=64),
             )
 
-        h0q = {(c, n): code_tiles([P, NB], "h0q%d%d" % (c, n)) for c in range(2) for n in range(2)}
-        wq = {(g, t): code_tiles([P, 3, 2, P], "wq%d%d" % (g, t)) for g in range(2) for t in range(4)}
-        wdq = {c: code_tiles([P, D], "wdq%d" % c) for c in range(2)}
-        h1q = {(g, n): code_tiles([P, NB], "h1q%d%d" % (g, n)) for g in range(2) for n in range(2)}
+        h0q = {(c, n): code_tiles("h0q%d%d" % (c, n)) for c in range(2) for n in range(2)}
+        wq = [code_tiles("wq%d" % m) for m in range(12)]
+        wdq = [code_tiles("wdq%d" % c) for c in range(2)]
+        h1q = {(g, n): code_tiles("h1q%d%d" % (g, n)) for g in range(2) for n in range(2)}
 
-        def leave_psum(eng, dst, src):
+        def job_moving(src, c, dst):
+            words = src[:].bitcast(F32)
+            return ([[[words[:, 2 * b + a, 256 * c + P * v : 256 * c + P * (v + 1)] for v in range(2)] for a in range(2)] for b in range(2)], dst)
+
+        def job_weights(m):
+            return ([[[wraw[2 * m + b][:].bitcast(F32)[:, 256 * c + P * v : 256 * c + P * (v + 1)] for v in range(2)] for c in range(2)] for b in range(2)], wq[m])
+
+        jobs = [job_moving(h0raw[0], 0, h0q[(0, 0)]), job_moving(h0raw[0], 1, h0q[(1, 0)])]
+        jobs += [job_weights(m) for m in range(W_FIRST // 2)]
+        jobs += [job_moving(h0raw[1], 0, h0q[(0, 1)]), job_moving(h0raw[1], 1, h0q[(1, 1)])]
+        jobs += [job_weights(m) for m in range(W_FIRST // 2, 12)]
+        jobs += [job_moving(wdraw, c, wdq[c]) for c in range(2)]
+        live = {}
+
+        def job_transposes(j):
+            banks = []
+            for b in range(2):
+                bank = psum.tile([P, 2, 2, P], F32, name="tb", tag="bank")
+                banks.append(bank)
+                for i in range(2):
+                    for v in range(2):
+                        nc.tensor.transpose(out=bank[:, i, v, :], in_=jobs[j][0][b][i][v], identity=ident[:])
+            grp = stage.tile([P, 2048], BF16, name="grp", tag="grp", bufs=4, align_bytes=64)
+            live[j] = (banks, grp)
+
+        def job_copy(j, b, eng):
+            banks, grp = live[j]
+            dst = grp[:].bitcast(F32).rearrange("p (b i r v) -> p b i r v", b=2, i=2, v=2)[:, b]
+            src = banks[b][:].rearrange("p i v r -> p i r v")
             if eng == "s":
                 nc.scalar.copy(out=dst, in_=src)
             else:
                 nc.vector.tensor_copy(out=dst, in_=src)
 
-        def convert_moving(src, c, dst, engines):
-            words = src[:].bitcast(F32)
-            grp = stage.tile([P, 2048], BF16, name="grp2", tag="grp2", align_bytes=64)
-            grp_w = grp[:].bitcast(F32).rearrange("p (b a r v) -> p b a r v", b=2, a=2, v=2)
-            banks = []
-            for b in range(2):
-                bank = psum.tile([P, 2, 2, P], F32, name="bank", tag="bank")
-                banks.append(bank)
-                for a in range(2):
-                    for v in range(2):
-                        lo = 256 * c + 128 * v
-                        nc.tensor.transpose(out=bank[:, a, v, :], in_=words[:, 2 * b + a, lo : lo + P], identity=ident[:])
-            for b in range(2):
-                leave_psum(engines[b], grp_w[:, b], banks[b][:].rearrange("p a v r -> p a r v"))
-            nc.vector.quantize_mx(out=dst[0][:].bitcast(FP8X4), scales=dst[1][:], in_=grp[:])
-
-        def convert_weights(g, t, engines):
-            u, e = divmod(t, 2)
-            banks = []
-            for gi in range(3):
-                words = wraw[(gi, g, u)][:].bitcast(F32)
-                bank = psum.tile([P, 2, 2, P], F32, name="bank", tag="bank")
-                banks.append(bank)
-                for c in range(2):
-                    for v in range(2):
-                        lo = 256 * c + 128 * v
-                        nc.tensor.transpose(out=bank[:, c, v, :], in_=words[:, e, lo : lo + P], identity=ident[:])
-            grps = []
-            for gi in range(3):
-                grp = stage.tile([P, 1024], BF16, name="grp1", tag="grp1", bufs=6, align_bytes=64)
-                grps.append(grp)
-                grp_w = grp[:].bitcast(F32).rearrange("p (c r v) -> p c r v", c=2, v=2)
-                leave_psum(engines[gi], grp_w, banks[gi][:].rearrange("p c v r -> p c r v"))
-            for gi in range(3):
-                nc.vector.quantize_mx(
-                    out=wq[(g, t)][0][:, gi].rearrange("p c r -> p (c r)").bitcast(FP8X4),
-                    scales=wq[(g, t)][1][:, gi].rearrange("p c r -> p (c r)"),
-                    in_=grps[gi][:],
-                )
+        def job_quantise(j):
+            dst = jobs[j][1]
+            nc.vector.quantize_mx(out=dst[0][:].bitcast(FP8X4), scales=dst[1][:], in_=live[j][1][:])
 
         bsum = consts.tile([P, 32], F32, name="bsum")
 
         def prepare_bias():
-            bank = psum.tile([P, 4, P], F32, name="bank", tag="bank")
+            bank = psum.tile([P, 4, P], F32, name="tb", tag="bank")
             nc.tensor.transpose(out=bank[:, 0, :], in_=brows[:].bitcast(F32), identity=ident[:])
             bw = consts.tile([P, 64], BF16, name="bw")
             nc.vector.tensor_copy(out=bw[:].bitcast(F32), in_=bank[:, 0, 0:32])
             nc.vector.tensor_tensor(out=bsum[:], in0=bw[:, 0:32], in1=bw[:, 32:64], op=ALU.add)
 
-        h1p = {}
+        units = UNITS
+        accs, gate, cc, tcc, h1p = {}, {}, {}, {}, {}
 
-        def unit(g, t, n):
-            accs = []
+        def mx(s):
+            g, t, n, lo_b, wid = units[s]
             for gi in range(3):
-                acc = psum.tile([P, NB], F32, name="acc", tag="bank")
-                accs.append(acc)
+                w = 3 * (4 * g + t) + gi
+                acc = psum.tile([P, wid], F32, name="acc%d" % gi, tag="bank")
+                accs[(s, gi)] = acc
                 for c in range(2):
+                    lo = 256 * (w % 2) + P * c
                     nc.tensor.matmul_mx(
                         out=acc[:],
-                        lhsT=wq[(g, t)][0][:, gi, c, :].bitcast(FP8X4),
-                        lhsT_scale=wq[(g, t)][1][:, gi, c, :],
-                        rhs=h0q[(c, n)][0][:].bitcast(FP8X4),
-                        rhs_scale=h0q[(c, n)][1][:],
+                        lhsT=wq[w // 2][0][:, lo : lo + P].bitcast(FP8X4),
+                        lhsT_scale=wq[w // 2][1][:, lo : lo + P],
+                        rhs=h0q[(c, n)][0][:, lo_b : lo_b + wid].bitcast(FP8X4),
+                        rhs_scale=h0q[(c, n)][1][:, lo_b : lo_b + wid],
                         start=(c == 0),
                         stop=(c == 1),
                     )
-            outs = []
-            for gi, func in enumerate((ACT.Sigmoid, ACT.Tanh, ACT.Sigmoid)):
-                col = GATES[gi] * 8 + g * 4 + t
-                o = act.tile([P, NB], F32, name="gate%d" % gi, tag="gate%d" % gi)
-                outs.append(o)
-                nc.scalar.activation(out=o[:], in_=accs[gi][:], func=func, bias=bsum[:, col : col + 1])
-            cc = act.tile([P, NB], F32, name="cc", tag="cc")
-            nc.vector.tensor_tensor(out=cc[:], in0=outs[0][:], in1=outs[1][:], op=ALU.mult)
-            tcc = act.tile([P, NB], F32, name="tcc", tag="tcc")
-            nc.scalar.activation(out=tcc[:], in_=cc[:], func=ACT.Tanh)
-            if t == 0:
-                h1p[n] = stage.tile([P, 4, NB], BF16, name="h1p", tag="h1p", bufs=4)
-            nc.vector.tensor_tensor(out=h1p[n][:, t, :], in0=outs[2][:], in1=tcc[:], op=ALU.mult)
-            if t == 3:
-                h1g = stage.tile([P, NB, 4], BF16, name="h1g", tag="h1g", bufs=2, align_bytes=64)
-                nc.vector.tensor_copy(
-                    out=h1g[:].rearrange("p (c i) t -> p c t i", i=4),
-                    in_=h1p[n][:].rearrange("p t (c i) -> p c t i", i=4),
-                )
-                nc.vector.quantize_mx(
-                    out=h1q[(g, n)][0][:].bitcast(FP8X4),
-                    scales=h1q[(g, n)][1][:],
-                    in_=h1g[:].rearrange("p c t -> p (c t)"),
+
+        def gate_act(s, gi):
+            g, t, n, lo_b, wid = units[s]
+            col = GATES[gi] * 8 + g * 4 + t
+            o = act.tile([P, wid], F32, name="gate%d" % gi, tag="gate%d" % gi)
+            gate[(s, gi)] = o
+            nc.scalar.activation(out=o[:], in_=accs[(s, gi)][:], func=(ACT.Tanh if gi == 1 else ACT.Sigmoid), bias=bsum[:, col : col + 1])
+
+        def cell(s):
+            cc[s] = act.tile([P, units[s][4]], F32, name="cc", tag="cc")
+            nc.vector.tensor_tensor(out=cc[s][:], in0=gate[(s, 0)][:], in1=gate[(s, 1)][:], op=ALU.mult)
+
+        def cell_tanh(s):
+            tcc[s] = act.tile([P, units[s][4]], F32, name="tcc", tag="tcc")
+            nc.scalar.activation(out=tcc[s][:], in_=cc[s][:], func=ACT.Tanh)
+
+        def hidden(s):
+            g, t, n, lo_b, wid = units[s]
+            if (g, n) not in h1p:
+                h1p[(g, n)] = stage.tile([P, 4, NB], BF16, name="h1p", tag="h1p", bufs=4)
+            nc.vector.tensor_tensor(out=h1p[(g, n)][:, t, lo_b : lo_b + wid], in0=gate[(s, 2)][:], in1=tcc[s][:], op=ALU.mult)
+
+        def regroup(g, n, lo_b, wid):
+            h1g = stage.tile([P, wid, 4], BF16, name="h1g", tag="h1g", bufs=2, align_bytes=64)
+            nc.vector.tensor_copy(
+                out=h1g[:].rearrange("p (c i) t -> p c t i", i=4),
+                in_=h1p[(g, n)][:, :, lo_b : lo_b + wid].rearrange("p t (c i) -> p c t i", i=4),
+            )
+            nc.vector.quantize_mx(
+                out=h1q[(g, n)][0][:, lo_b : lo_b + wid].bitcast(FP8X4),
+                scales=h1q[(g, n)][1][:, lo_b : lo_b + wid],
+                in_=h1g[:].rearrange("p c t -> p (c t)"),
+            )
+
+        dacc = {}
+
+        def decode_mx(n, a):
+            acc = psum.tile([P, D], F32, name="dacc", tag="bank")
+            dacc[(n, a)] = acc
+            for g in range(2):
+                nc.tensor.matmul_mx(
+                    out=acc[:],
+                    lhsT=h1q[(g, n)][0][:, P * a : P * (a + 1)].bitcast(FP8X4),
+                    lhsT_scale=h1q[(g, n)][1][:, P * a : P * (a + 1)],
+                    rhs=wdq[g][0][:].bitcast(FP8X4),
+                    rhs_scale=wdq[g][1][:],
+                    start=(g == 0),
+                    stop=(g == 1),
                 )
 
-        def decode(n):
+        def decode_out(n, a):
             view = out[NB * n : NB * (n + 1), :].rearrange("(r a) d -> r a d", a=4)
-            for a in range(4):
-                acc = psum.tile([P, D], F32, name="acc", tag="bank")
-                for g in range(2):
-                    nc.tensor.matmul_mx(
-                        out=acc[:],
-                        lhsT=h1q[(g, n)][0][:, P * a : P * (a + 1)].bitcast(FP8X4),
-                        lhsT_scale=h1q[(g, n)][1][:, P * a : P * (a + 1)],
-                        rhs=wdq[g][0][:].bitcast(FP8X4),
-                        rhs_scale=wdq[g][1][:],
-                        start=(g == 0),
-                        stop=(g == 1),
-                    )
-                res = act.tile([P, D], F32, name="res", tag="res", bufs=4)
-                nc.vector.tensor_tensor(out=res[:], in0=acc[:], in1=bdec[:], op=ALU.add)
-                nc.sync.dma_start(out=view[:, a, :], in_=res[:])
+            res = act.tile([P, D], F32, name="res", tag="res", bufs=4)
+            nc.vector.tensor_tensor(out=res[:], in0=dacc[(n, a)][:], in1=bdec[:], op=ALU.add)
+            nc.sync.dma_start(out=view[:, a, :], in_=res[:])
 
-        convert_moving(h0raw[0], 0, h0q[(0, 0)], "sv")
-        convert_moving(h0raw[0], 1, h0q[(1, 0)], "sv")
-        convert_weights(0, 0, "svs")
-        prepare_bias()
-        convert_moving(h0raw[1], 0, h0q[(0, 1)], "sv")
-        convert_moving(h0raw[1], 1, h0q[(1, 1)], "sv")
-        pairs = [(g, t) for g in range(2) for t in range(4)]
-        for i, (g, t) in enumerate(pairs):
-            if i + 1 < len(pairs):
-                convert_weights(pairs[i + 1][0], pairs[i + 1][1], "vsv")
-            if i in (5, 6):
-                convert_moving(wdraw, i - 5, wdq[i - 5], "sv")
-            for n in range(2):
-                unit(g, t, n)
-                if (g, t) == (1, 3):
-                    decode(n)
+        pending = []
+        with tc.manual_schedule():
+            for j in range(PRE):
+                job_transposes(j)
+                job_copy(j, 0, "s")
+                job_copy(j, 1, PRE_ENG[j])
+                if j == 0:
+                    prepare_bias()
+                job_quantise(j)
+            mx(0)
+            nu = len(units)
+            for s in range(0, nu + 5):
+                j = s + PRE
+                now = [x for x in pending if x[0] <= s][:2]
+                pending = [x for x in pending if x not in now]
+                if j < 18:
+                    job_transposes(j)
+                if s + 1 < nu:
+                    mx(s + 1)
+                for s0, n, a in now:
+                    decode_mx(n, a)
+                if s < nu:
+                    gate_act(s, 0)
+                    gate_act(s, 1)
+                if j < 18:
+                    job_copy(j, 0, COPY_ENG[s])
+                    job_copy(j, 1, "v")
+                if s < nu:
+                    cell(s)
+                if 0 <= s - 1 < nu:
+                    cell_tanh(s - 1)
+                if s < nu:
+                    gate_act(s, 2)
+                if 0 <= s - 1 < nu:
+                    hidden(s - 1)
+                if j < 18:
+                    job_quantise(j)
+                for s0, n, a in now:
+                    decode_out(n, a)
+                if s in RG0:
+                    regroup(0, RG0[s], 0, 512)
+                if 0 <= s - 1 < nu and units[s - 1][1] == 3 and units[s - 1][0] == 1:
+                    g, t, n, lo_b, wid = units[s - 1]
+                    regroup(g, n, lo_b, wid)
+                    pending += [(s + DLAG if s < nu else s, n, a) for a in range(lo_b // P, (lo_b + wid) // P)]

@@ -210,7 +210,7 @@ def tile_lstmbaseline_pb_kernel(tc, h0, W_ih1, b_ih1, b_hh1, W_dec, b_dec, out):
             nc.sync.dma_start(out=view[:, a, :], in_=res[:])
 
         pending = []
-        with tc.manual_schedule():
+        if True:
             for j in range(PRE):
                 job_transposes(j)
                 job_copy(j, 0, "s")

@@ -18,13 +18,15 @@ ALU = mybir.AluOpType
 P = 128
 NB = 512
 GATES = (0, 2, 3)
-W_FIRST = 4
-UNITS = [(0, t, n, 0, 512) for t in range(4) for n in range(2)] + [(1, t, 0, 0, 512) for t in range(4)] + [(1, t, 1, 0, 512) for t in range(3)] + [(1, 3, 1, 0, 256), (1, 3, 1, 256, 256)]
-PRE = 6
-PRE_ENG = "vsssss"
-COPY_ENG = "svsvsvsvsvsv"
-RG0 = {11: 0, 14: 1}
-DLAG = 2
+W_FIRST = 6
+UNITS = [(0, t, n, 0, 512) for tt in (0, 2) for n in range(2) for t in (tt, tt + 1)] + [(1, t, 0, 0, 512) for t in range(4)] + [(1, t, 1, 0, 512) for t in range(3)] + [(1, 3, 1, 0, 256), (1, 3, 1, 256, 256)]
+PRE = 5
+PRE_ENG = "vssssss"
+DOUBLE = 3
+S_MOD = 3
+S_PAR = 1
+RG0 = {9: 0, 11: 1}
+DLAG = 1
 
 
 def tile_lstmbaseline_pb_kernel(tc, h0, W_ih1, b_ih1, b_hh1, W_dec, b_dec, out):
@@ -210,7 +212,8 @@ def tile_lstmbaseline_pb_kernel(tc, h0, W_ih1, b_ih1, b_hh1, W_dec, b_dec, out):
             nc.sync.dma_start(out=view[:, a, :], in_=res[:])
 
         pending = []
-        if True:
+        flying = []
+        with tc.manual_schedule():
             for j in range(PRE):
                 job_transposes(j)
                 job_copy(j, 0, "s")
@@ -220,21 +223,17 @@ def tile_lstmbaseline_pb_kernel(tc, h0, W_ih1, b_ih1, b_hh1, W_dec, b_dec, out):
                 job_quantise(j)
             mx(0)
             nu = len(units)
+            nxt = PRE
             for s in range(0, nu + 5):
-                j = s + PRE
-                now = [x for x in pending if x[0] <= s][:2]
-                pending = [x for x in pending if x not in now]
-                if j < 18:
+                todo = [j for j in range(nxt, nxt + (2 if s < DOUBLE else 1)) if j < 18]
+                nxt += len(todo)
+                for j in todo:
                     job_transposes(j)
-                if s + 1 < nu:
-                    mx(s + 1)
-                for s0, n, a in now:
-                    decode_mx(n, a)
                 if s < nu:
                     gate_act(s, 0)
                     gate_act(s, 1)
-                if j < 18:
-                    job_copy(j, 0, COPY_ENG[s])
+                for i, j in enumerate(todo):
+                    job_copy(j, 0, "s" if j % S_MOD != S_PAR else "v")
                     job_copy(j, 1, "v")
                 if s < nu:
                     cell(s)
@@ -244,9 +243,9 @@ def tile_lstmbaseline_pb_kernel(tc, h0, W_ih1, b_ih1, b_hh1, W_dec, b_dec, out):
                     gate_act(s, 2)
                 if 0 <= s - 1 < nu:
                     hidden(s - 1)
-                if j < 18:
+                for j in todo:
                     job_quantise(j)
-                for s0, n, a in now:
+                for n, a in flying:
                     decode_out(n, a)
                 if s in RG0:
                     regroup(0, RG0[s], 0, 512)
@@ -254,3 +253,9 @@ def tile_lstmbaseline_pb_kernel(tc, h0, W_ih1, b_ih1, b_hh1, W_dec, b_dec, out):
                     g, t, n, lo_b, wid = units[s - 1]
                     regroup(g, n, lo_b, wid)
                     pending += [(s + DLAG if s < nu else s, n, a) for a in range(lo_b // P, (lo_b + wid) // P)]
+                if s + 1 < nu:
+                    mx(s + 1)
+                flying = [(n, a) for s0, n, a in pending if s0 <= s][:2]
+                pending = [x for x in pending if (x[1], x[2]) not in flying]
+                for n, a in flying:
+                    decode_mx(n, a)

@@ -23,8 +23,8 @@ UNITS = [(0, t, n, 0, 512) for tt in (0, 2) for n in range(2) for t in (tt, tt +
 PRE = 5
 PRE_ENG = "vssssss"
 DOUBLE = 3
-S_MOD = 3
-S_PAR = 1
+S_MOD = 99
+S_PAR = 98
 RG0 = {9: 0, 11: 1}
 DLAG = 1
 

@@ -16,17 +16,19 @@ ACT = mybir.ActivationFunctionType
 ALU = mybir.AluOpType
 
 P = 128
-NB = 512
-GATES = (0, 2, 3)
-W_FIRST = 6
-UNITS = [(0, t, n, 0, 512) for tt in (0, 2) for n in range(2) for t in (tt, tt + 1)] + [(1, t, 0, 0, 512) for t in range(4)] + [(1, t, 1, 0, 512) for t in range(3)] + [(1, 3, 1, 0, 256), (1, 3, 1, 256, 256)]
-PRE = 5
-PRE_ENG = "vssssss"
-DOUBLE = 3
-S_MOD = 99
-S_PAR = 98
-RG0 = {9: 0, 11: 1}
-DLAG = 1
+HALF = 512
+GATE_BLOCK = (0, 2, 3)
+I_GATE, G_GATE, O_GATE = 0, 1, 2
+
+UNITS = (
+    [(0, t, n, 0, HALF) for pair in (0, 2) for n in range(2) for t in (pair, pair + 1)]
+    + [(1, t, 0, 0, HALF) for t in range(4)]
+    + [(1, t, 1, 0, HALF) for t in range(3)]
+    + [(1, 3, 1, 0, HALF // 2), (1, 3, 1, HALF // 2, HALF // 2)]
+)
+FIRST_WEIGHT_JOBS = 3
+PROLOGUE_JOBS = 2 + FIRST_WEIGHT_JOBS
+DOUBLE_SLOTS = 3
 
 
 def tile_lstmbaseline_pb_kernel(tc, h0, W_ih1, b_ih1, b_hh1, W_dec, b_dec, out):
@@ -34,7 +36,7 @@ def tile_lstmbaseline_pb_kernel(tc, h0, W_ih1, b_ih1, b_hh1, W_dec, b_dec, out):
     with ExitStack() as ctx:
         consts = ctx.enter_context(tc.tile_pool(name="consts", bufs=1))
         raw = ctx.enter_context(tc.tile_pool(name="raw", bufs=1))
-        stage = ctx.enter_context(tc.tile_pool(name="stage", bufs=3))
+        stage = ctx.enter_context(tc.tile_pool(name="stage", bufs=4))
         codes = ctx.enter_context(tc.tile_pool(name="codes", bufs=1))
         act = ctx.enter_context(tc.tile_pool(name="act", bufs=3))
         psum = ctx.enter_context(tc.psum_pool(name="psum", bufs=8))
@@ -44,218 +46,254 @@ def tile_lstmbaseline_pb_kernel(tc, h0, W_ih1, b_ih1, b_hh1, W_dec, b_dec, out):
         warm = consts.tile([P, 2], F32, name="warm")
         nc.vector.memset(warm[:], 0.0)
         nc.scalar.activation(out=warm[:, 1:2], in_=warm[:, 0:1], func=ACT.Sigmoid)
-        brows = consts.tile([P, 256], BF16, name="brows")
-        nc.vector.memset(brows[:], 0.0)
-        nc.scalar.dma_start(out=brows[0:16, :], in_=b_ih1.rearrange("(r q) -> r q", q=256))
-        nc.scalar.dma_start(out=brows[16:32, :], in_=b_hh1.rearrange("(r q) -> r q", q=256))
+        bias_rows = consts.tile([P, 256], BF16, name="bias_rows")
+        nc.vector.memset(bias_rows[:], 0.0)
+        nc.scalar.dma_start(out=bias_rows[0:16, :], in_=b_ih1.rearrange("(r q) -> r q", q=256))
+        nc.scalar.dma_start(out=bias_rows[16:32, :], in_=b_hh1.rearrange("(r q) -> r q", q=256))
 
-        h0raw = [raw.tile([P, 4, H], BF16, name="h0raw%d" % n) for n in range(2)]
-        wraw = [raw.tile([P, H], BF16, name="wraw%d" % w) for w in range(24)]
-        wdraw = raw.tile([P, 4, H], BF16, name="wdraw")
+        h0_raw = [raw.tile([P, 4, H], BF16, name="h0_raw%d" % n) for n in range(2)]
+        w_raw = [raw.tile([P, H], BF16, name="w_raw%d" % w) for w in range(24)]
+        wd_raw = raw.tile([P, 4, H], BF16, name="wd_raw")
         bdec = consts.tile([P, D], BF16, name="bdec")
 
         def load_h0(n):
-            view = h0[NB * n : NB * (n + 1), :].rearrange("(r a) k -> r a k", a=4)
-            for b in range(2):
-                nc.sync.dma_start(out=h0raw[n][:, 2 * b : 2 * b + 2, :], in_=view[:, 2 * b : 2 * b + 2, :])
+            rows = h0[HALF * n : HALF * (n + 1), :].rearrange("(r a) k -> r a k", a=4)
+            for pair in (0, 2):
+                nc.sync.dma_start(out=h0_raw[n][:, pair : pair + 2, :], in_=rows[:, pair : pair + 2, :])
 
-        def load_w(w):
-            q, gi = divmod(w, 3)
-            g, t = divmod(q, 4)
+        def load_weight_tile(w):
+            group_tile, gate = divmod(w, 3)
+            g, t = divmod(group_tile, 4)
             u, e = divmod(t, 2)
-            base = GATES[gi] * H + 512 * g + 256 * u
-            nc.sync.dma_start(out=wraw[w][:], in_=W_ih1[base : base + 256, :].rearrange("(p e) k -> p e k", e=2)[:, e, :])
+            first = GATE_BLOCK[gate] * H + 512 * g + 256 * u
+            rows = W_ih1[first : first + 256, :].rearrange("(p e) k -> p e k", e=2)
+            nc.sync.dma_start(out=w_raw[w][:], in_=rows[:, e, :])
 
         load_h0(0)
-        for w in range(W_FIRST):
-            load_w(w)
+        for w in range(2 * FIRST_WEIGHT_JOBS):
+            load_weight_tile(w)
         load_h0(1)
-        for w in range(W_FIRST, 24):
-            load_w(w)
-        wd_view = W_dec.rearrange("(a r) k -> r a k", r=P)
-        for b in range(2):
-            nc.sync.dma_start(out=wdraw[:, 2 * b : 2 * b + 2, :], in_=wd_view[:, 2 * b : 2 * b + 2, :])
+        for w in range(2 * FIRST_WEIGHT_JOBS, 24):
+            load_weight_tile(w)
+        wd_rows = W_dec.rearrange("(a r) k -> r a k", r=P)
+        for pair in (0, 2):
+            nc.sync.dma_start(out=wd_raw[:, pair : pair + 2, :], in_=wd_rows[:, pair : pair + 2, :])
         nc.sync.dma_start(out=bdec[:], in_=b_dec.partition_broadcast(P))
 
-        def code_tiles(name):
+        def quantised(name):
             return (
-                codes.tile([P, NB], U32, name=name + "c", align_bytes=64),
-                codes.tile([P, NB], U8, name=name + "s", align_bytes=64),
+                codes.tile([P, HALF], U32, name=name + "_words", align_bytes=64),
+                codes.tile([P, HALF], U8, name=name + "_scales", align_bytes=64),
             )
 
-        h0q = {(c, n): code_tiles("h0q%d%d" % (c, n)) for c in range(2) for n in range(2)}
-        wq = [code_tiles("wq%d" % m) for m in range(12)]
-        wdq = [code_tiles("wdq%d" % c) for c in range(2)]
-        h1q = {(g, n): code_tiles("h1q%d%d" % (g, n)) for g in range(2) for n in range(2)}
+        h0_q = {(c, n): quantised("h0_q%d%d" % (c, n)) for c in range(2) for n in range(2)}
+        w_q = [quantised("w_q%d" % m) for m in range(12)]
+        wd_q = [quantised("wd_q%d" % c) for c in range(2)]
+        h1_q = {(g, n): quantised("h1_q%d%d" % (g, n)) for g in range(2) for n in range(2)}
 
-        def job_moving(src, c, dst):
+        def words_of_pass(tile_words, c):
+            return [tile_words[:, 256 * c + P * v : 256 * c + P * (v + 1)] for v in range(2)]
+
+        def moving_job(src, c, dst):
             words = src[:].bitcast(F32)
-            return ([[[words[:, 2 * b + a, 256 * c + P * v : 256 * c + P * (v + 1)] for v in range(2)] for a in range(2)] for b in range(2)], dst)
+            return ([[words_of_pass(words[:, 2 * bank + i, :], c) for i in range(2)] for bank in range(2)], dst)
 
-        def job_weights(m):
-            return ([[[wraw[2 * m + b][:].bitcast(F32)[:, 256 * c + P * v : 256 * c + P * (v + 1)] for v in range(2)] for c in range(2)] for b in range(2)], wq[m])
+        def weight_job(m):
+            return ([[words_of_pass(w_raw[2 * m + bank][:].bitcast(F32), c) for c in range(2)] for bank in range(2)], w_q[m])
 
-        jobs = [job_moving(h0raw[0], 0, h0q[(0, 0)]), job_moving(h0raw[0], 1, h0q[(1, 0)])]
-        jobs += [job_weights(m) for m in range(W_FIRST // 2)]
-        jobs += [job_moving(h0raw[1], 0, h0q[(0, 1)]), job_moving(h0raw[1], 1, h0q[(1, 1)])]
-        jobs += [job_weights(m) for m in range(W_FIRST // 2, 12)]
-        jobs += [job_moving(wdraw, c, wdq[c]) for c in range(2)]
-        live = {}
+        jobs = [moving_job(h0_raw[0], c, h0_q[(c, 0)]) for c in range(2)]
+        jobs += [weight_job(m) for m in range(FIRST_WEIGHT_JOBS)]
+        jobs += [moving_job(h0_raw[1], c, h0_q[(c, 1)]) for c in range(2)]
+        jobs += [weight_job(m) for m in range(FIRST_WEIGHT_JOBS, 12)]
+        jobs += [moving_job(wd_raw, c, wd_q[c]) for c in range(2)]
+        job_tiles = {}
 
         def job_transposes(j):
             banks = []
-            for b in range(2):
-                bank = psum.tile([P, 2, 2, P], F32, name="tb", tag="bank")
-                banks.append(bank)
+            for bank in range(2):
+                tp = psum.tile([P, 2, 2, P], F32, name="tp", tag="bank")
+                banks.append(tp)
                 for i in range(2):
                     for v in range(2):
-                        nc.tensor.transpose(out=bank[:, i, v, :], in_=jobs[j][0][b][i][v], identity=ident[:])
-            grp = stage.tile([P, 2048], BF16, name="grp", tag="grp", bufs=4, align_bytes=64)
-            live[j] = (banks, grp)
+                        nc.tensor.transpose(out=tp[:, i, v, :], in_=jobs[j][0][bank][i][v], identity=ident[:])
+            grouped = stage.tile([P, 4 * HALF], BF16, name="grouped", tag="grouped", align_bytes=64)
+            job_tiles[j] = (banks, grouped)
 
-        def job_copy(j, b, eng):
-            banks, grp = live[j]
-            dst = grp[:].bitcast(F32).rearrange("p (b i r v) -> p b i r v", b=2, i=2, v=2)[:, b]
-            src = banks[b][:].rearrange("p i v r -> p i r v")
-            if eng == "s":
+        def job_copy(j, bank, engine):
+            banks, grouped = job_tiles[j]
+            dst = grouped[:].bitcast(F32).rearrange("p (b i r v) -> p b i r v", b=2, i=2, v=2)[:, bank]
+            src = banks[bank][:].rearrange("p i v r -> p i r v")
+            if engine == "scalar":
                 nc.scalar.copy(out=dst, in_=src)
             else:
                 nc.vector.tensor_copy(out=dst, in_=src)
 
         def job_quantise(j):
-            dst = jobs[j][1]
-            nc.vector.quantize_mx(out=dst[0][:].bitcast(FP8X4), scales=dst[1][:], in_=live[j][1][:])
+            words, scales = jobs[j][1]
+            nc.vector.quantize_mx(out=words[:].bitcast(FP8X4), scales=scales[:], in_=job_tiles[j][1][:])
 
-        bsum = consts.tile([P, 32], F32, name="bsum")
+        bias = consts.tile([P, 32], F32, name="bias")
 
         def prepare_bias():
-            bank = psum.tile([P, 4, P], F32, name="tb", tag="bank")
-            nc.tensor.transpose(out=bank[:, 0, :], in_=brows[:].bitcast(F32), identity=ident[:])
-            bw = consts.tile([P, 64], BF16, name="bw")
-            nc.vector.tensor_copy(out=bw[:].bitcast(F32), in_=bank[:, 0, 0:32])
-            nc.vector.tensor_tensor(out=bsum[:], in0=bw[:, 0:32], in1=bw[:, 32:64], op=ALU.add)
+            tp = psum.tile([P, 4, P], F32, name="tp", tag="bank")
+            nc.tensor.transpose(out=tp[:, 0, :], in_=bias_rows[:].bitcast(F32), identity=ident[:])
+            both = consts.tile([P, 64], BF16, name="both")
+            nc.vector.tensor_copy(out=both[:].bitcast(F32), in_=tp[:, 0, 0:32])
+            nc.vector.tensor_tensor(out=bias[:], in0=both[:, 0:32], in1=both[:, 32:64], op=ALU.add)
 
-        units = UNITS
-        accs, gate, cc, tcc, h1p = {}, {}, {}, {}, {}
+        sums, gates, cells, cell_tanhs, h1_planes, h1_grouped = {}, {}, {}, {}, {}, {}
 
-        def mx(s):
-            g, t, n, lo_b, wid = units[s]
-            for gi in range(3):
-                w = 3 * (4 * g + t) + gi
-                acc = psum.tile([P, wid], F32, name="acc%d" % gi, tag="bank")
-                accs[(s, gi)] = acc
+        def gate_matmuls(s):
+            g, t, n, first, cols = UNITS[s]
+            for gate in range(3):
+                w = 3 * (4 * g + t) + gate
+                acc = psum.tile([P, cols], F32, name="acc", tag="bank")
+                sums[(s, gate)] = acc
                 for c in range(2):
                     lo = 256 * (w % 2) + P * c
                     nc.tensor.matmul_mx(
                         out=acc[:],
-                        lhsT=wq[w // 2][0][:, lo : lo + P].bitcast(FP8X4),
-                        lhsT_scale=wq[w // 2][1][:, lo : lo + P],
-                        rhs=h0q[(c, n)][0][:, lo_b : lo_b + wid].bitcast(FP8X4),
-                        rhs_scale=h0q[(c, n)][1][:, lo_b : lo_b + wid],
+                        lhsT=w_q[w // 2][0][:, lo : lo + P].bitcast(FP8X4),
+                        lhsT_scale=w_q[w // 2][1][:, lo : lo + P],
+                        rhs=h0_q[(c, n)][0][:, first : first + cols].bitcast(FP8X4),
+                        rhs_scale=h0_q[(c, n)][1][:, first : first + cols],
                         start=(c == 0),
                         stop=(c == 1),
                     )
 
-        def gate_act(s, gi):
-            g, t, n, lo_b, wid = units[s]
-            col = GATES[gi] * 8 + g * 4 + t
-            o = act.tile([P, wid], F32, name="gate%d" % gi, tag="gate%d" % gi)
-            gate[(s, gi)] = o
-            nc.scalar.activation(out=o[:], in_=accs[(s, gi)][:], func=(ACT.Tanh if gi == 1 else ACT.Sigmoid), bias=bsum[:, col : col + 1])
+        def gate_activation(s, gate):
+            g, t, n, first, cols = UNITS[s]
+            column = 8 * GATE_BLOCK[gate] + 4 * g + t
+            res = act.tile([P, cols], F32, name="gate%d" % gate, tag="gate%d" % gate)
+            gates[(s, gate)] = res
+            nc.scalar.activation(
+                out=res[:],
+                in_=sums[(s, gate)][:],
+                func=(ACT.Tanh if gate == G_GATE else ACT.Sigmoid),
+                bias=bias[:, column : column + 1],
+            )
 
         def cell(s):
-            cc[s] = act.tile([P, units[s][4]], F32, name="cc", tag="cc")
-            nc.vector.tensor_tensor(out=cc[s][:], in0=gate[(s, 0)][:], in1=gate[(s, 1)][:], op=ALU.mult)
+            cells[s] = act.tile([P, UNITS[s][4]], F32, name="cell", tag="cell")
+            nc.vector.tensor_tensor(out=cells[s][:], in0=gates[(s, I_GATE)][:], in1=gates[(s, G_GATE)][:], op=ALU.mult)
 
         def cell_tanh(s):
-            tcc[s] = act.tile([P, units[s][4]], F32, name="tcc", tag="tcc")
-            nc.scalar.activation(out=tcc[s][:], in_=cc[s][:], func=ACT.Tanh)
+            cell_tanhs[s] = act.tile([P, UNITS[s][4]], F32, name="cell_tanh", tag="cell_tanh")
+            nc.scalar.activation(out=cell_tanhs[s][:], in_=cells[s][:], func=ACT.Tanh)
 
         def hidden(s):
-            g, t, n, lo_b, wid = units[s]
-            if (g, n) not in h1p:
-                h1p[(g, n)] = stage.tile([P, 4, NB], BF16, name="h1p", tag="h1p", bufs=4)
-            nc.vector.tensor_tensor(out=h1p[(g, n)][:, t, lo_b : lo_b + wid], in0=gate[(s, 2)][:], in1=tcc[s][:], op=ALU.mult)
+            g, t, n, first, cols = UNITS[s]
+            if (g, n) not in h1_planes:
+                h1_planes[(g, n)] = stage.tile([P, 4, HALF], BF16, name="h1_planes", tag="h1_planes")
+            nc.vector.tensor_tensor(
+                out=h1_planes[(g, n)][:, t, first : first + cols],
+                in0=gates[(s, O_GATE)][:],
+                in1=cell_tanhs[s][:],
+                op=ALU.mult,
+            )
 
-        def regroup(g, n, lo_b, wid):
-            h1g = stage.tile([P, wid, 4], BF16, name="h1g", tag="h1g", bufs=2, align_bytes=64)
+        def regroup(g, n, first, cols):
+            grouped = stage.tile([P, cols, 4], BF16, name="h1_grouped", tag="h1_grouped", bufs=2, align_bytes=64)
+            h1_grouped[(g, n, first)] = grouped
             nc.vector.tensor_copy(
-                out=h1g[:].rearrange("p (c i) t -> p c t i", i=4),
-                in_=h1p[(g, n)][:, :, lo_b : lo_b + wid].rearrange("p t (c i) -> p c t i", i=4),
+                out=grouped[:].rearrange("p (c i) t -> p c t i", i=4),
+                in_=h1_planes[(g, n)][:, :, first : first + cols].rearrange("p t (c i) -> p c t i", i=4),
             )
+
+        def hidden_quantise(g, n, first, cols):
             nc.vector.quantize_mx(
-                out=h1q[(g, n)][0][:, lo_b : lo_b + wid].bitcast(FP8X4),
-                scales=h1q[(g, n)][1][:, lo_b : lo_b + wid],
-                in_=h1g[:].rearrange("p c t -> p (c t)"),
+                out=h1_q[(g, n)][0][:, first : first + cols].bitcast(FP8X4),
+                scales=h1_q[(g, n)][1][:, first : first + cols],
+                in_=h1_grouped[(g, n, first)][:].rearrange("p c t -> p (c t)"),
             )
 
-        dacc = {}
+        decoded = {}
 
-        def decode_mx(n, a):
-            acc = psum.tile([P, D], F32, name="dacc", tag="bank")
-            dacc[(n, a)] = acc
+        def decoder_matmuls(n, a):
+            acc = psum.tile([P, D], F32, name="dec", tag="bank")
+            decoded[(n, a)] = acc
             for g in range(2):
                 nc.tensor.matmul_mx(
                     out=acc[:],
-                    lhsT=h1q[(g, n)][0][:, P * a : P * (a + 1)].bitcast(FP8X4),
-                    lhsT_scale=h1q[(g, n)][1][:, P * a : P * (a + 1)],
-                    rhs=wdq[g][0][:].bitcast(FP8X4),
-                    rhs_scale=wdq[g][1][:],
+                    lhsT=h1_q[(g, n)][0][:, P * a : P * (a + 1)].bitcast(FP8X4),
+                    lhsT_scale=h1_q[(g, n)][1][:, P * a : P * (a + 1)],
+                    rhs=wd_q[g][0][:].bitcast(FP8X4),
+                    rhs_scale=wd_q[g][1][:],
                     start=(g == 0),
                     stop=(g == 1),
                 )
 
-        def decode_out(n, a):
-            view = out[NB * n : NB * (n + 1), :].rearrange("(r a) d -> r a d", a=4)
+        def decoder_store(n, a):
+            rows = out[HALF * n : HALF * (n + 1), :].rearrange("(r a) d -> r a d", a=4)
             res = act.tile([P, D], F32, name="res", tag="res", bufs=4)
-            nc.vector.tensor_tensor(out=res[:], in0=dacc[(n, a)][:], in1=bdec[:], op=ALU.add)
-            nc.sync.dma_start(out=view[:, a, :], in_=res[:])
+            nc.vector.tensor_tensor(out=res[:], in0=decoded[(n, a)][:], in1=bdec[:], op=ALU.add)
+            nc.sync.dma_start(out=rows[:, a, :], in_=res[:])
 
-        pending = []
-        flying = []
+        def quantise_groups(groups):
+            ready = []
+            for g, n, first, cols in groups:
+                hidden_quantise(g, n, first, cols)
+                if g == 1:
+                    ready += [(n, a) for a in range(first // P, (first + cols) // P)]
+            return ready
+
+        n_units = len(UNITS)
         with tc.manual_schedule():
-            for j in range(PRE):
+            for j in range(PROLOGUE_JOBS):
                 job_transposes(j)
-                job_copy(j, 0, "s")
-                job_copy(j, 1, PRE_ENG[j])
+                job_copy(j, 0, "scalar")
+                job_copy(j, 1, "vector")
                 if j == 0:
                     prepare_bias()
                 job_quantise(j)
-            mx(0)
-            nu = len(units)
-            nxt = PRE
-            for s in range(0, nu + 5):
-                todo = [j for j in range(nxt, nxt + (2 if s < DOUBLE else 1)) if j < 18]
-                nxt += len(todo)
-                for j in todo:
+            gate_matmuls(0)
+            next_job = PROLOGUE_JOBS
+            late_halves = [0, 1]
+            regrouped = []
+            waiting = []
+            in_psum = []
+            for s in range(n_units + 3):
+                slot_jobs = list(range(next_job, min(next_job + (2 if s < DOUBLE_SLOTS else 1), len(jobs))))
+                next_job += len(slot_jobs)
+                has_unit = s < n_units
+                has_previous = 1 <= s <= n_units
+                for j in slot_jobs:
                     job_transposes(j)
-                if s < nu:
-                    gate_act(s, 0)
-                    gate_act(s, 1)
-                for i, j in enumerate(todo):
-                    job_copy(j, 0, "s" if j % S_MOD != S_PAR else "v")
-                    job_copy(j, 1, "v")
-                if s < nu:
+                if has_unit:
+                    gate_activation(s, I_GATE)
+                    gate_activation(s, G_GATE)
+                for j in slot_jobs:
+                    job_copy(j, 0, "vector" if j % 3 == 2 else "scalar")
+                    job_copy(j, 1, "vector")
+                waiting += quantise_groups(regrouped)
+                regrouped = []
+                if has_unit:
                     cell(s)
-                if 0 <= s - 1 < nu:
+                if has_previous:
                     cell_tanh(s - 1)
-                if s < nu:
-                    gate_act(s, 2)
-                if 0 <= s - 1 < nu:
+                if has_unit:
+                    gate_activation(s, O_GATE)
+                if has_previous:
                     hidden(s - 1)
-                for j in todo:
+                for j in slot_jobs:
                     job_quantise(j)
-                for n, a in flying:
-                    decode_out(n, a)
-                if s in RG0:
-                    regroup(0, RG0[s], 0, 512)
-                if 0 <= s - 1 < nu and units[s - 1][1] == 3 and units[s - 1][0] == 1:
-                    g, t, n, lo_b, wid = units[s - 1]
-                    regroup(g, n, lo_b, wid)
-                    pending += [(s + DLAG if s < nu else s, n, a) for a in range(lo_b // P, (lo_b + wid) // P)]
-                if s + 1 < nu:
-                    mx(s + 1)
-                flying = [(n, a) for s0, n, a in pending if s0 <= s][:2]
-                pending = [x for x in pending if (x[1], x[2]) not in flying]
-                for n, a in flying:
-                    decode_mx(n, a)
+                for n, a in in_psum:
+                    decoder_store(n, a)
+                if late_halves and not slot_jobs:
+                    regroup(0, late_halves[0], 0, HALF)
+                    regrouped.append((0, late_halves[0], 0, HALF))
+                    late_halves = late_halves[1:]
+                if has_previous:
+                    g, t, n, first, cols = UNITS[s - 1]
+                    if g == 1 and t == 3:
+                        regroup(g, n, first, cols)
+                        regrouped.append((g, n, first, cols))
+                if not has_unit:
+                    waiting += quantise_groups(regrouped)
+                    regrouped = []
+                if s + 1 < n_units:
+                    gate_matmuls(s + 1)
+                in_psum = waiting[:2]
+                waiting = waiting[2:]
+                for n, a in in_psum:
+                    decoder_matmuls(n, a)

@@ -36,7 +36,7 @@ def tile_lstmbaseline_pb_kernel(tc, h0, W_ih1, b_ih1, b_hh1, W_dec, b_dec, out):
     with ExitStack() as ctx:
         consts = ctx.enter_context(tc.tile_pool(name="consts", bufs=1))
         raw = ctx.enter_context(tc.tile_pool(name="raw", bufs=1))
-        stage = ctx.enter_context(tc.tile_pool(name="stage", bufs=4))
+        stage = ctx.enter_context(tc.tile_pool(name="stage", bufs=3))
         codes = ctx.enter_context(tc.tile_pool(name="codes", bufs=1))
         act = ctx.enter_context(tc.tile_pool(name="act", bufs=3))
         psum = ctx.enter_context(tc.psum_pool(name="psum", bufs=8))
@@ -46,14 +46,14 @@ def tile_lstmbaseline_pb_kernel(tc, h0, W_ih1, b_ih1, b_hh1, W_dec, b_dec, out):
         warm = consts.tile([P, 2], F32, name="warm")
         nc.vector.memset(warm[:], 0.0)
         nc.scalar.activation(out=warm[:, 1:2], in_=warm[:, 0:1], func=ACT.Sigmoid)
-        bias_rows = consts.tile([P, 256], BF16, name="bias_rows")
+        bias_rows = consts.tile([P, 256], BF16, name="brows")
         nc.vector.memset(bias_rows[:], 0.0)
         nc.scalar.dma_start(out=bias_rows[0:16, :], in_=b_ih1.rearrange("(r q) -> r q", q=256))
         nc.scalar.dma_start(out=bias_rows[16:32, :], in_=b_hh1.rearrange("(r q) -> r q", q=256))
 
-        h0_raw = [raw.tile([P, 4, H], BF16, name="h0_raw%d" % n) for n in range(2)]
-        w_raw = [raw.tile([P, H], BF16, name="w_raw%d" % w) for w in range(24)]
-        wd_raw = raw.tile([P, 4, H], BF16, name="wd_raw")
+        h0_raw = [raw.tile([P, 4, H], BF16, name="h0raw%d" % n) for n in range(2)]
+        w_raw = [raw.tile([P, H], BF16, name="wraw%d" % w) for w in range(24)]
+        wd_raw = raw.tile([P, 4, H], BF16, name="wdraw")
         bdec = consts.tile([P, D], BF16, name="bdec")
 
         def load_h0(n):
@@ -82,14 +82,14 @@ def tile_lstmbaseline_pb_kernel(tc, h0, W_ih1, b_ih1, b_hh1, W_dec, b_dec, out):
 
         def quantised(name):
             return (
-                codes.tile([P, HALF], U32, name=name + "_words", align_bytes=64),
-                codes.tile([P, HALF], U8, name=name + "_scales", align_bytes=64),
+                codes.tile([P, HALF], U32, name=name + "c", align_bytes=64),
+                codes.tile([P, HALF], U8, name=name + "s", align_bytes=64),
             )
 
-        h0_q = {(c, n): quantised("h0_q%d%d" % (c, n)) for c in range(2) for n in range(2)}
-        w_q = [quantised("w_q%d" % m) for m in range(12)]
-        wd_q = [quantised("wd_q%d" % c) for c in range(2)]
-        h1_q = {(g, n): quantised("h1_q%d%d" % (g, n)) for g in range(2) for n in range(2)}
+        h0_q = {(c, n): quantised("h0q%d%d" % (c, n)) for c in range(2) for n in range(2)}
+        w_q = [quantised("wq%d" % m) for m in range(12)]
+        wd_q = [quantised("wdq%d" % c) for c in range(2)]
+        h1_q = {(g, n): quantised("h1q%d%d" % (g, n)) for g in range(2) for n in range(2)}
 
         def words_of_pass(tile_words, c):
             return [tile_words[:, 256 * c + P * v : 256 * c + P * (v + 1)] for v in range(2)]
@@ -111,12 +111,12 @@ def tile_lstmbaseline_pb_kernel(tc, h0, W_ih1, b_ih1, b_hh1, W_dec, b_dec, out):
         def job_transposes(j):
             banks = []
             for bank in range(2):
-                tp = psum.tile([P, 2, 2, P], F32, name="tp", tag="bank")
+                tp = psum.tile([P, 2, 2, P], F32, name="tb", tag="bank")
                 banks.append(tp)
                 for i in range(2):
                     for v in range(2):
                         nc.tensor.transpose(out=tp[:, i, v, :], in_=jobs[j][0][bank][i][v], identity=ident[:])
-            grouped = stage.tile([P, 4 * HALF], BF16, name="grouped", tag="grouped", align_bytes=64)
+            grouped = stage.tile([P, 4 * HALF], BF16, name="grp", tag="grp", bufs=3, align_bytes=64)
             job_tiles[j] = (banks, grouped)
 
         def job_copy(j, bank, engine):
@@ -132,22 +132,27 @@ def tile_lstmbaseline_pb_kernel(tc, h0, W_ih1, b_ih1, b_hh1, W_dec, b_dec, out):
             words, scales = jobs[j][1]
             nc.vector.quantize_mx(out=words[:].bitcast(FP8X4), scales=scales[:], in_=job_tiles[j][1][:])
 
-        bias = consts.tile([P, 32], F32, name="bias")
+        bias = consts.tile([P, 32], F32, name="bsum")
 
         def prepare_bias():
-            tp = psum.tile([P, 4, P], F32, name="tp", tag="bank")
+            tp = psum.tile([P, 4, P], F32, name="tb", tag="bank")
             nc.tensor.transpose(out=tp[:, 0, :], in_=bias_rows[:].bitcast(F32), identity=ident[:])
-            both = consts.tile([P, 64], BF16, name="both")
+            both = consts.tile([P, 64], BF16, name="bw")
             nc.vector.tensor_copy(out=both[:].bitcast(F32), in_=tp[:, 0, 0:32])
             nc.vector.tensor_tensor(out=bias[:], in0=both[:, 0:32], in1=both[:, 32:64], op=ALU.add)
 
-        sums, gates, cells, cell_tanhs, h1_planes, h1_grouped = {}, {}, {}, {}, {}, {}
+        sums, gates, cells, out_gates, cell_tanhs, h1_grouped = {}, {}, {}, {}, {}, {}
+
+        def group_tile(tiles, tag, g, n):
+            if (g, n) not in tiles:
+                tiles[(g, n)] = stage.tile([P, 4, HALF], F32, name=tag, tag=tag, bufs=3)
+            return tiles[(g, n)]
 
         def gate_matmuls(s):
             g, t, n, first, cols = UNITS[s]
             for gate in range(3):
                 w = 3 * (4 * g + t) + gate
-                acc = psum.tile([P, cols], F32, name="acc", tag="bank")
+                acc = psum.tile([P, cols], F32, name="acc%d" % gate, tag="bank")
                 sums[(s, gate)] = acc
                 for c in range(2):
                     lo = 256 * (w % 2) + P * c
@@ -164,53 +169,48 @@ def tile_lstmbaseline_pb_kernel(tc, h0, W_ih1, b_ih1, b_hh1, W_dec, b_dec, out):
         def gate_activation(s, gate):
             g, t, n, first, cols = UNITS[s]
             column = 8 * GATE_BLOCK[gate] + 4 * g + t
-            res = act.tile([P, cols], F32, name="gate%d" % gate, tag="gate%d" % gate)
-            gates[(s, gate)] = res
+            if gate == O_GATE:
+                res = group_tile(out_gates, "so4", g, n)[:, t, first : first + cols]
+            else:
+                res = act.tile([P, cols], F32, name="gate%d" % gate, tag="gate%d" % gate)[:]
+                gates[(s, gate)] = res
             nc.scalar.activation(
-                out=res[:],
+                out=res,
                 in_=sums[(s, gate)][:],
                 func=(ACT.Tanh if gate == G_GATE else ACT.Sigmoid),
                 bias=bias[:, column : column + 1],
             )
 
         def cell(s):
-            cells[s] = act.tile([P, UNITS[s][4]], F32, name="cell", tag="cell")
-            nc.vector.tensor_tensor(out=cells[s][:], in0=gates[(s, I_GATE)][:], in1=gates[(s, G_GATE)][:], op=ALU.mult)
+            cells[s] = act.tile([P, UNITS[s][4]], F32, name="cc", tag="cc")
+            nc.vector.tensor_tensor(out=cells[s][:], in0=gates[(s, I_GATE)], in1=gates[(s, G_GATE)], op=ALU.mult)
 
         def cell_tanh(s):
-            cell_tanhs[s] = act.tile([P, UNITS[s][4]], F32, name="cell_tanh", tag="cell_tanh")
-            nc.scalar.activation(out=cell_tanhs[s][:], in_=cells[s][:], func=ACT.Tanh)
-
-        def hidden(s):
             g, t, n, first, cols = UNITS[s]
-            if (g, n) not in h1_planes:
-                h1_planes[(g, n)] = stage.tile([P, 4, HALF], BF16, name="h1_planes", tag="h1_planes")
+            res = group_tile(cell_tanhs, "tc4", g, n)[:, t, first : first + cols]
+            nc.scalar.activation(out=res, in_=cells[s][:], func=ACT.Tanh)
+
+        def hidden_product(g, n, a):
+            grouped = stage.tile([P, P, 4], BF16, name="h1g", tag="h1g", bufs=4, align_bytes=64)
+            h1_grouped[(g, n, a)] = grouped
             nc.vector.tensor_tensor(
-                out=h1_planes[(g, n)][:, t, first : first + cols],
-                in0=gates[(s, O_GATE)][:],
-                in1=cell_tanhs[s][:],
+                out=grouped[:].rearrange("p (c i) t -> p c t i", i=4),
+                in0=out_gates[(g, n)][:, :, P * a : P * (a + 1)].rearrange("p t (c i) -> p c t i", i=4),
+                in1=cell_tanhs[(g, n)][:, :, P * a : P * (a + 1)].rearrange("p t (c i) -> p c t i", i=4),
                 op=ALU.mult,
             )
 
-        def regroup(g, n, first, cols):
-            grouped = stage.tile([P, cols, 4], BF16, name="h1_grouped", tag="h1_grouped", bufs=2, align_bytes=64)
-            h1_grouped[(g, n, first)] = grouped
-            nc.vector.tensor_copy(
-                out=grouped[:].rearrange("p (c i) t -> p c t i", i=4),
-                in_=h1_planes[(g, n)][:, :, first : first + cols].rearrange("p t (c i) -> p c t i", i=4),
-            )
-
-        def hidden_quantise(g, n, first, cols):
+        def hidden_quantise(g, n, a):
             nc.vector.quantize_mx(
-                out=h1_q[(g, n)][0][:, first : first + cols].bitcast(FP8X4),
-                scales=h1_q[(g, n)][1][:, first : first + cols],
-                in_=h1_grouped[(g, n, first)][:].rearrange("p c t -> p (c t)"),
+                out=h1_q[(g, n)][0][:, P * a : P * (a + 1)].bitcast(FP8X4),
+                scales=h1_q[(g, n)][1][:, P * a : P * (a + 1)],
+                in_=h1_grouped[(g, n, a)][:].rearrange("p c t -> p (c t)"),
             )
 
         decoded = {}
 
         def decoder_matmuls(n, a):
-            acc = psum.tile([P, D], F32, name="dec", tag="bank")
+            acc = psum.tile([P, D], F32, name="dacc", tag="bank")
             decoded[(n, a)] = acc
             for g in range(2):
                 nc.tensor.matmul_mx(
@@ -229,27 +229,18 @@ def tile_lstmbaseline_pb_kernel(tc, h0, W_ih1, b_ih1, b_hh1, W_dec, b_dec, out):
             nc.vector.tensor_tensor(out=res[:], in0=decoded[(n, a)][:], in1=bdec[:], op=ALU.add)
             nc.sync.dma_start(out=rows[:, a, :], in_=res[:])
 
-        def quantise_groups(groups):
-            ready = []
-            for g, n, first, cols in groups:
-                hidden_quantise(g, n, first, cols)
-                if g == 1:
-                    ready += [(n, a) for a in range(first // P, (first + cols) // P)]
-            return ready
-
         n_units = len(UNITS)
         with tc.manual_schedule():
             for j in range(PROLOGUE_JOBS):
                 job_transposes(j)
                 job_copy(j, 0, "scalar")
-                job_copy(j, 1, "vector")
+                job_copy(j, 1, "vector" if j < 2 else "scalar")
                 if j == 0:
                     prepare_bias()
                 job_quantise(j)
             gate_matmuls(0)
             next_job = PROLOGUE_JOBS
-            late_halves = [0, 1]
-            regrouped = []
+            chunks = []
             waiting = []
             in_psum = []
             for s in range(n_units + 3):
@@ -263,10 +254,8 @@ def tile_lstmbaseline_pb_kernel(tc, h0, W_ih1, b_ih1, b_hh1, W_dec, b_dec, out):
                     gate_activation(s, I_GATE)
                     gate_activation(s, G_GATE)
                 for j in slot_jobs:
-                    job_copy(j, 0, "vector" if j % 3 == 2 else "scalar")
+                    job_copy(j, 0, "vector" if j % 2 == 1 else "scalar")
                     job_copy(j, 1, "vector")
-                waiting += quantise_groups(regrouped)
-                regrouped = []
                 if has_unit:
                     cell(s)
                 if has_previous:
@@ -274,26 +263,27 @@ def tile_lstmbaseline_pb_kernel(tc, h0, W_ih1, b_ih1, b_hh1, W_dec, b_dec, out):
                 if has_unit:
                     gate_activation(s, O_GATE)
                 if has_previous:
-                    hidden(s - 1)
+                    g, t, n, first, cols = UNITS[s - 1]
+                    if t == 3:
+                        chunks += [(g, n, a) for a in range(first // P, (first + cols) // P)]
+                quota = 1 if slot_jobs else 2
+                taken = chunks[:quota]
+                chunks = chunks[quota:]
+                for g, n, a in taken:
+                    hidden_product(g, n, a)
                 for j in slot_jobs:
                     job_quantise(j)
                 for n, a in in_psum:
                     decoder_store(n, a)
-                if late_halves and not slot_jobs:
-                    regroup(0, late_halves[0], 0, HALF)
-                    regrouped.append((0, late_halves[0], 0, HALF))
-                    late_halves = late_halves[1:]
-                if has_previous:
-                    g, t, n, first, cols = UNITS[s - 1]
-                    if g == 1 and t == 3:
-                        regroup(g, n, first, cols)
-                        regrouped.append((g, n, first, cols))
-                if not has_unit:
-                    waiting += quantise_groups(regrouped)
-                    regrouped = []
+                for g, n, a in taken:
+                    hidden_quantise(g, n, a)
+                fresh = [(n, a) for g, n, a in taken if g == 1]
                 if s + 1 < n_units:
                     gate_matmuls(s + 1)
+                if not has_unit:
+                    waiting += fresh
+                    fresh = []
                 in_psum = waiting[:2]
-                waiting = waiting[2:]
+                waiting = waiting[2:] + fresh
                 for n, a in in_psum:
                     decoder_matmuls(n, a)

@@ -235,9 +235,9 @@ def tile_lstmbaseline_pb_kernel(tc, h0, W_ih1, b_ih1, b_hh1, W_dec, b_dec, out):
                 job_transposes(j)
                 job_copy(j, 0, "scalar")
                 job_copy(j, 1, "vector" if j < 2 else "scalar")
-                if j == 0:
-                    prepare_bias()
                 job_quantise(j)
+                if j == 2:
+                    prepare_bias()
             gate_matmuls(0)
             next_job = PROLOGUE_JOBS
             chunks = []

@@ -28,6 +28,7 @@ UNITS = (
 )
 FIRST_WEIGHT_JOBS = 3
 PROLOGUE_JOBS = 2 + FIRST_WEIGHT_JOBS
+WARM_UP_MATMULS = 6
 DOUBLE_SLOTS = 3
 
 
@@ -230,7 +231,12 @@ def tile_lstmbaseline_pb_kernel(tc, h0, W_ih1, b_ih1, b_hh1, W_dec, b_dec, out):
             nc.sync.dma_start(out=rows[:, a, :], in_=res[:])
 
         n_units = len(UNITS)
+        zeros = consts.tile([P, HALF], BF16, name="zeros")
+        nc.vector.memset(zeros[:], 0.0)
         with tc.manual_schedule():
+            idle = psum.tile([P, HALF], F32, name="idle", tag="bank")
+            for i in range(WARM_UP_MATMULS):
+                nc.tensor.matmul(out=idle[:], lhsT=zeros[:, 0:P], rhs=zeros[:], start=True, stop=True)
             for j in range(PROLOGUE_JOBS):
                 job_transposes(j)
                 job_copy(j, 0, "scalar")

@@ -28,7 +28,7 @@ UNITS = (
 )
 FIRST_WEIGHT_JOBS = 3
 PROLOGUE_JOBS = 2 + FIRST_WEIGHT_JOBS
-WARM_UP_MATMULS = 6
+WARM_UP_MATMULS = 5
 DOUBLE_SLOTS = 3
 
 
@@ -108,6 +108,11 @@ def tile_lstmbaseline_pb_kernel(tc, h0, W_ih1, b_ih1, b_hh1, W_dec, b_dec, out):
         jobs += [weight_job(m) for m in range(FIRST_WEIGHT_JOBS, 12)]
         jobs += [moving_job(wd_raw, c, wd_q[c]) for c in range(2)]
         job_tiles = {}
+
+        def keep_clock(count):
+            idle = psum.tile([P, HALF], F32, name="idle", tag="bank")
+            for i in range(count):
+                nc.tensor.matmul(out=idle[:], lhsT=zeros[:, 0:P], rhs=zeros[:], start=True, stop=True)
 
         def job_transposes(j):
             banks = []
@@ -234,11 +239,11 @@ def tile_lstmbaseline_pb_kernel(tc, h0, W_ih1, b_ih1, b_hh1, W_dec, b_dec, out):
         zeros = consts.tile([P, HALF], BF16, name="zeros")
         nc.vector.memset(zeros[:], 0.0)
         with tc.manual_schedule():
-            idle = psum.tile([P, HALF], F32, name="idle", tag="bank")
-            for i in range(WARM_UP_MATMULS):
-                nc.tensor.matmul(out=idle[:], lhsT=zeros[:, 0:P], rhs=zeros[:], start=True, stop=True)
+            keep_clock(WARM_UP_MATMULS)
             for j in range(PROLOGUE_JOBS):
                 job_transposes(j)
+                if j + 1 < PROLOGUE_JOBS:
+                    keep_clock(2)
                 job_copy(j, 0, "scalar")
                 job_copy(j, 1, "vector" if j < 2 else "scalar")
                 job_quantise(j)

@@ -83,8 +83,8 @@ def tile_lstmbaseline_pb_kernel(tc, h0, W_ih1, b_ih1, b_hh1, W_dec, b_dec, out):
 
         def quantised(name):
             return (
-                codes.tile([P, HALF], U32, name=name + "c", align_bytes=64),
-                codes.tile([P, HALF], U8, name=name + "s", align_bytes=64),
+                codes.tile([P, HALF], U32, name=name + "c", align_bytes=256),
+                codes.tile([P, HALF], U8, name=name + "s", align_bytes=256),
             )
 
         h0_q = {(c, n): quantised("h0q%d%d" % (c, n)) for c in range(2) for n in range(2)}
@@ -296,5 +296,7 @@ def tile_lstmbaseline_pb_kernel(tc, h0, W_ih1, b_ih1, b_hh1, W_dec, b_dec, out):
                     fresh = []
                 in_psum = waiting[:2]
                 waiting = waiting[2:] + fresh
+                if s == n_units:
+                    keep_clock(4)
                 for n, a in in_psum:
                     decoder_matmuls(n, a)

from contextlib import ExitStack

import concourse.mybir as mybir
from concourse.masks import make_identity

B, H, D = 1024, 1024, 512
FLOPS = 2 * B * H * (3 * H + D)
BYTES = 2 * (B * H + 3 * H * H + 6 * H + D * H + D) + 4 * B * D

F32 = mybir.dt.float32
BF16 = mybir.dt.bfloat16
U32 = mybir.dt.uint32
U8 = mybir.dt.uint8
FP8X4 = mybir.dt.float8_e4m3fn_x4
ACT = mybir.ActivationFunctionType
ALU = mybir.AluOpType

P = 128
HALF = 512
GATE_BLOCK = (0, 2, 3)
I_GATE, G_GATE, O_GATE = 0, 1, 2

UNITS = (
    [(0, t, n, 0, HALF) for pair in (0, 2) for n in range(2) for t in (pair, pair + 1)]
    + [(1, t, 0, 0, HALF) for t in range(4)]
    + [(1, t, 1, 0, HALF) for t in range(3)]
    + [(1, 3, 1, 0, HALF // 2), (1, 3, 1, HALF // 2, HALF // 2)]
)
FIRST_WEIGHT_JOBS = 3
PROLOGUE_JOBS = 2 + FIRST_WEIGHT_JOBS
WARM_UP_MATMULS = 5
DOUBLE_SLOTS = 3


def tile_lstmbaseline_pb_kernel(tc, h0, W_ih1, b_ih1, b_hh1, W_dec, b_dec, out):
    nc = tc.nc
    with ExitStack() as ctx:
        consts = ctx.enter_context(tc.tile_pool(name="consts", bufs=1))
        raw = ctx.enter_context(tc.tile_pool(name="raw", bufs=1))
        stage = ctx.enter_context(tc.tile_pool(name="stage", bufs=3))
        codes = ctx.enter_context(tc.tile_pool(name="codes", bufs=1))
        act = ctx.enter_context(tc.tile_pool(name="act", bufs=3))
        psum = ctx.enter_context(tc.psum_pool(name="psum", bufs=8))

        ident = consts.tile([P, P], F32, name="ident")
        make_identity(nc, ident[:])
        warm = consts.tile([P, 2], F32, name="warm")
        nc.vector.memset(warm[:], 0.0)
        nc.scalar.activation(out=warm[:, 1:2], in_=warm[:, 0:1], func=ACT.Sigmoid)
        bias_rows = consts.tile([P, 256], BF16, name="brows")
        nc.vector.memset(bias_rows[:], 0.0)
        nc.scalar.dma_start(out=bias_rows[0:16, :], in_=b_ih1.rearrange("(r q) -> r q", q=256))
        nc.scalar.dma_start(out=bias_rows[16:32, :], in_=b_hh1.rearrange("(r q) -> r q", q=256))

        h0_raw = [raw.tile([P, 4, H], BF16, name="h0raw%d" % n) for n in range(2)]
        w_raw = [raw.tile([P, H], BF16, name="wraw%d" % w) for w in range(24)]
        wd_raw = raw.tile([P, 4, H], BF16, name="wdraw")
        bdec = consts.tile([P, D], BF16, name="bdec")

        def load_h0(n):
            rows = h0[HALF * n : HALF * (n + 1), :].rearrange("(r a) k -> r a k", a=4)
            for pair in (0, 2):
                nc.sync.dma_start(out=h0_raw[n][:, pair : pair + 2, :], in_=rows[:, pair : pair + 2, :])

        def load_weight_tile(w):
            group_tile, gate = divmod(w, 3)
            g, t = divmod(group_tile, 4)
            u, e = divmod(t, 2)
            first = GATE_BLOCK[gate] * H + 512 * g + 256 * u
            rows = W_ih1[first : first + 256, :].rearrange("(p e) k -> p e k", e=2)
            nc.sync.dma_start(out=w_raw[w][:], in_=rows[:, e, :])

        load_h0(0)
        for w in range(2 * FIRST_WEIGHT_JOBS):
            load_weight_tile(w)
        load_h0(1)
        for w in range(2 * FIRST_WEIGHT_JOBS, 24):
            load_weight_tile(w)
        wd_rows = W_dec.rearrange("(a r) k -> r a k", r=P)
        for pair in (0, 2):
            nc.sync.dma_start(out=wd_raw[:, pair : pair + 2, :], in_=wd_rows[:, pair : pair + 2, :])
        nc.sync.dma_start(out=bdec[:], in_=b_dec.partition_broadcast(P))

        def quantised(name):
            return (
                codes.tile([P, HALF], U32, name=name + "c", align_bytes=256),
                codes.tile([P, HALF], U8, name=name + "s", align_bytes=256),
            )

        h0_q = {(c, n): quantised("h0q%d%d" % (c, n)) for c in range(2) for n in range(2)}
        w_q = [quantised("wq%d" % m) for m in range(12)]
        wd_q = [quantised("wdq%d" % c) for c in range(2)]
        h1_q = {(g, n): quantised("h1q%d%d" % (g, n)) for g in range(2) for n in range(2)}

        def words_of_pass(tile_words, c):
            return [tile_words[:, 256 * c + P * v : 256 * c + P * (v + 1)] for v in range(2)]

        def moving_job(src, c, dst):
            words = src[:].bitcast(F32)
            return ([[words_of_pass(words[:, 2 * bank + i, :], c) for i in range(2)] for bank in range(2)], dst)

        def weight_job(m):
            return ([[words_of_pass(w_raw[2 * m + bank][:].bitcast(F32), c) for c in range(2)] for bank in range(2)], w_q[m])

        jobs = [moving_job(h0_raw[0], c, h0_q[(c, 0)]) for c in range(2)]
        jobs += [weight_job(m) for m in range(FIRST_WEIGHT_JOBS)]
        jobs += [moving_job(h0_raw[1], c, h0_q[(c, 1)]) for c in range(2)]
        jobs += [weight_job(m) for m in range(FIRST_WEIGHT_JOBS, 12)]
        jobs += [moving_job(wd_raw, c, wd_q[c]) for c in range(2)]
        job_tiles = {}

        def keep_clock(count):
            idle = psum.tile([P, HALF], F32, name="idle", tag="bank")
            for i in range(count):
                nc.tensor.matmul(out=idle[:], lhsT=zeros[:, 0:P], rhs=zeros[:], start=True, stop=True)

        def job_transposes(j):
            banks = []
            for bank in range(2):
                tp = psum.tile([P, 2, 2, P], F32, name="tb", tag="bank")
                banks.append(tp)
                for i in range(2):
                    for v in range(2):
                        nc.tensor.transpose(out=tp[:, i, v, :], in_=jobs[j][0][bank][i][v], identity=ident[:])
            grouped = stage.tile([P, 4 * HALF], BF16, name="grp", tag="grp", bufs=3, align_bytes=64)
            job_tiles[j] = (banks, grouped)

        def job_copy(j, bank, engine):
            banks, grouped = job_tiles[j]
            dst = grouped[:].bitcast(F32).rearrange("p (b i r v) -> p b i r v", b=2, i=2, v=2)[:, bank]
            src = banks[bank][:].rearrange("p i v r -> p i r v")
            if engine == "scalar":
                nc.scalar.copy(out=dst, in_=src)
            else:
                nc.vector.tensor_copy(out=dst, in_=src)

        def job_quantise(j):
            words, scales = jobs[j][1]
            nc.vector.quantize_mx(out=words[:].bitcast(FP8X4), scales=scales[:], in_=job_tiles[j][1][:])

        bias = consts.tile([P, 32], F32, name="bsum")

        def prepare_bias():
            tp = psum.tile([P, 4, P], F32, name="tb", tag="bank")
            nc.tensor.transpose(out=tp[:, 0, :], in_=bias_rows[:].bitcast(F32), identity=ident[:])
            both = consts.tile([P, 64], BF16, name="bw")
            nc.vector.tensor_copy(out=both[:].bitcast(F32), in_=tp[:, 0, 0:32])
            nc.vector.tensor_tensor(out=bias[:], in0=both[:, 0:32], in1=both[:, 32:64], op=ALU.add)

        sums, gates, cells, out_gates, cell_tanhs, h1_grouped = {}, {}, {}, {}, {}, {}

        def group_tile(tiles, tag, g, n):
            if (g, n) not in tiles:
                tiles[(g, n)] = stage.tile([P, 4, HALF], F32, name=tag, tag=tag, bufs=3)
            return tiles[(g, n)]

        def gate_matmuls(s):
            g, t, n, first, cols = UNITS[s]
            for gate in range(3):
                w = 3 * (4 * g + t) + gate
                acc = psum.tile([P, cols], F32, name="acc%d" % gate, tag="bank")
                sums[(s, gate)] = acc
                for c in range(2):
                    lo = 256 * (w % 2) + P * c
                    nc.tensor.matmul_mx(
                        out=acc[:],
                        lhsT=w_q[w // 2][0][:, lo : lo + P].bitcast(FP8X4),
                        lhsT_scale=w_q[w // 2][1][:, lo : lo + P],
                        rhs=h0_q[(c, n)][0][:, first : first + cols].bitcast(FP8X4),
                        rhs_scale=h0_q[(c, n)][1][:, first : first + cols],
                        start=(c == 0),
                        stop=(c == 1),
                    )

        def gate_activation(s, gate):
            g, t, n, first, cols = UNITS[s]
            column = 8 * GATE_BLOCK[gate] + 4 * g + t
            if gate == O_GATE:
                res = group_tile(out_gates, "so4", g, n)[:, t, first : first + cols]
            else:
                res = act.tile([P, cols], F32, name="gate%d" % gate, tag="gate%d" % gate)[:]
                gates[(s, gate)] = res
            nc.scalar.activation(
                out=res,
                in_=sums[(s, gate)][:],
                func=(ACT.Tanh if gate == G_GATE else ACT.Sigmoid),
                bias=bias[:, column : column + 1],
            )

        def cell(s):
            cells[s] = act.tile([P, UNITS[s][4]], F32, name="cc", tag="cc")
            nc.vector.tensor_tensor(out=cells[s][:], in0=gates[(s, I_GATE)], in1=gates[(s, G_GATE)], op=ALU.mult)

        def cell_tanh(s):
            g, t, n, first, cols = UNITS[s]
            res = group_tile(cell_tanhs, "tc4", g, n)[:, t, first : first + cols]
            nc.scalar.activation(out=res, in_=cells[s][:], func=ACT.Tanh)

        def hidden_product(g, n, a):
            grouped = stage.tile([P, P, 4], BF16, name="h1g", tag="h1g", bufs=4, align_bytes=64)
            h1_grouped[(g, n, a)] = grouped
            nc.vector.tensor_tensor(
                out=grouped[:].rearrange("p (c i) t -> p c t i", i=4),
                in0=out_gates[(g, n)][:, :, P * a : P * (a + 1)].rearrange("p t (c i) -> p c t i", i=4),
                in1=cell_tanhs[(g, n)][:, :, P * a : P * (a + 1)].rearrange("p t (c i) -> p c t i", i=4),
                op=ALU.mult,
            )

        def hidden_quantise(g, n, a):
            nc.vector.quantize_mx(
                out=h1_q[(g, n)][0][:, P * a : P * (a + 1)].bitcast(FP8X4),
                scales=h1_q[(g, n)][1][:, P * a : P * (a + 1)],
                in_=h1_grouped[(g, n, a)][:].rearrange("p c t -> p (c t)"),
            )

        decoded = {}

        def decoder_matmuls(n, a):
            acc = psum.tile([P, D], F32, name="dacc", tag="bank")
            decoded[(n, a)] = acc
            for g in range(2):
                nc.tensor.matmul_mx(
                    out=acc[:],
                    lhsT=h1_q[(g, n)][0][:, P * a : P * (a + 1)].bitcast(FP8X4),
                    lhsT_scale=h1_q[(g, n)][1][:, P * a : P * (a + 1)],
                    rhs=wd_q[g][0][:].bitcast(FP8X4),
                    rhs_scale=wd_q[g][1][:],
                    start=(g == 0),
                    stop=(g == 1),
                )

        def decoder_store(n, a):
            rows = out[HALF * n : HALF * (n + 1), :].rearrange("(r a) d -> r a d", a=4)
            res = act.tile([P, D], F32, name="res", tag="res", bufs=4)
            nc.vector.tensor_tensor(out=res[:], in0=decoded[(n, a)][:], in1=bdec[:], op=ALU.add)
            nc.sync.dma_start(out=rows[:, a, :], in_=res[:])

        n_units = len(UNITS)
        zeros = consts.tile([P, HALF], BF16, name="zeros")
        nc.vector.memset(zeros[:], 0.0)
        with tc.manual_schedule():
            keep_clock(WARM_UP_MATMULS)
            for j in range(PROLOGUE_JOBS):
                job_transposes(j)
                if j + 1 < PROLOGUE_JOBS:
                    keep_clock(2)
                job_copy(j, 0, "scalar")
                job_copy(j, 1, "vector" if j < 2 else "scalar")
                job_quantise(j)
                if j == 2:
                    prepare_bias()
            gate_matmuls(0)
            next_job = PROLOGUE_JOBS
            chunks = []
            waiting = []
            in_psum = []
            for s in range(n_units + 3):
                slot_jobs = list(range(next_job, min(next_job + (2 if s < DOUBLE_SLOTS else 1), len(jobs))))
                next_job += len(slot_jobs)
                has_unit = s < n_units
                has_previous = 1 <= s <= n_units
                for j in slot_jobs:
                    job_transposes(j)
                if has_unit:
                    gate_activation(s, I_GATE)
                    gate_activation(s, G_GATE)
                for j in slot_jobs:
                    job_copy(j, 0, "vector" if j % 2 == 1 else "scalar")
                    job_copy(j, 1, "vector")
                if has_unit:
                    cell(s)
                if has_previous:
                    cell_tanh(s - 1)
                if has_unit:
                    gate_activation(s, O_GATE)
                if has_previous:
                    g, t, n, first, cols = UNITS[s - 1]
                    if t == 3:
                        chunks += [(g, n, a) for a in range(first // P, (first + cols) // P)]
                quota = 1 if slot_jobs else 2
                taken = chunks[:quota]
                chunks = chunks[quota:]
                for g, n, a in taken:
                    hidden_product(g, n, a)
                for j in slot_jobs:
                    job_quantise(j)
                for n, a in in_psum:
                    decoder_store(n, a)
                for g, n, a in taken:
                    hidden_quantise(g, n, a)
                fresh = [(n, a) for g, n, a in taken if g == 1]
                if s + 1 < n_units:
                    gate_matmuls(s + 1)
                if not has_unit:
                    waiting += fresh
                    fresh = []
                in_psum = waiting[:2]
                waiting = waiting[2:] + fresh
                if s == n_units:
                    keep_clock(4)
                for n, a in in_psum:
                    decoder_matmuls(n, a)
